import numpy as np
import ml_dtypes


def mxq(x, axis, fmt="e4m3"):
    dtype, down = {"e4m3": (ml_dtypes.float8_e4m3fn, 7), "e5m2": (ml_dtypes.float8_e5m2, 14)}[fmt]
    v = np.moveaxis(np.asarray(x, np.float32).astype(ml_dtypes.bfloat16).astype(np.float64), axis, -1)
    blocks = v.reshape(v.shape[:-1] + (-1, 32))
    amax = np.abs(blocks).max(-1, keepdims=True)
    byte = np.maximum(np.where(amax > 0, np.frexp(amax)[1] - 1 + 127, 0) - down, 1)
    scale = np.exp2(byte - 127.0)
    codes = (blocks / scale).astype(np.float32).astype(dtype).astype(np.float64)
    return np.moveaxis((codes * scale).reshape(v.shape), -1, axis)


WIDE = False


def mx_kscale(k):
    if not WIDE:
        return np.ones(k)
    levels = np.array([10, -10, 5, -5, 0])
    a = np.random.permutation(np.resize(levels, k // 512 * 4)).reshape(k // 512, 4)
    idx = np.arange(k)
    return np.exp2(a[idx // 512, idx % 128 // 32])


BF16 = ml_dtypes.bfloat16


def bf(x):
    return np.asarray(x, np.float32).astype(BF16)


def f64(x):
    return np.asarray(x).astype(np.float64)


B, IN, OUT = 16384, 512, 256
MU = 0.25


def setup_inputs():
    s = mx_kscale(IN)
    x = np.random.standard_normal((B, IN)) + MU * np.random.standard_normal(IN)
    return {"x": bf(x * s),
            "wa": bf(np.random.standard_normal((OUT, IN)) / MU / s),
            "wb": bf(np.random.standard_normal((OUT, IN)) / MU),
            "wc": bf(np.random.standard_normal((OUT, IN)) * 12.0 / s),
            "wd": bf(np.random.standard_normal((OUT, IN))),
            "weight": bf(np.random.standard_normal((OUT, IN)) / np.sqrt(IN) / s)}


def reference(x, wa, wb, wc, wd, weight):
    x_ = f64(x)
    y_ = mxq(x_, 1, "e4m3") @ mxq(f64(weight), 1, "e4m3").T
    corr = mxq(y_, 0, "e4m3").T @ mxq(x_, 0, "e4m3")
    dw = (x_.mean(axis=0)[None, :] * f64(wa)
          + y_.mean(axis=0)[:, None] * f64(wb)
          + corr * f64(wc) / B
          + f64(wd))
    return dw

@@ -1,0 +1,267 @@
+from contextlib import ExitStack
+
+import concourse.mybir as mybir
+from concourse.masks import make_identity
+
+F32 = mybir.dt.float32
+BF16 = mybir.dt.bfloat16
+U32 = mybir.dt.uint32
+U8 = mybir.dt.uint8
+FP8X4 = mybir.dt.float8_e4m3fn_x4
+ADD = mybir.AluOpType.add
+MULT = mybir.AluOpType.mult
+
+P = 128
+PACK = 4
+K_PASS = P * PACK
+BATCH, N_IN, N_OUT = 16384, 512, 256
+PASSES = BATCH // K_PASS
+OUT_HALVES = N_OUT // P
+IN_CHUNKS = N_IN // P
+PAIR = 2
+LOADS_AHEAD = 4
+
+FLOPS = 2 * 2 * BATCH * N_IN * N_OUT
+
+
+def tile_hebbianlinear_pa_k_kernel(tc, x, wa, wb, wc, wd, weight, out):
+    nc = tc.nc
+    x_passes = x.rearrange("(c p j) i -> c p j i", p=P, j=PACK)
+
+    with ExitStack() as ctx:
+        const = ctx.enter_context(tc.tile_pool(name="const", bufs=1))
+        raw_pool = ctx.enter_context(tc.tile_pool(name="raw", bufs=LOADS_AHEAD + 2))
+        two = ctx.enter_context(tc.tile_pool(name="two", bufs=2))
+        three = ctx.enter_context(tc.tile_pool(name="three", bufs=3))
+        psum = ctx.enter_context(tc.psum_pool(name="psum", bufs=1))
+        ctx.enter_context(tc.manual_schedule())
+
+        raw = {}
+        xa_codes, xa_scales = {}, {}
+        xb_codes, xb_scales = {}, {}
+        y_grouped = {}
+        y_codes, y_scales = {}, {}
+
+        def load(c):
+            raw_c = raw_pool.tile([P, PACK, N_IN], BF16)
+            nc.sync.dma_start(out=raw_c[:], in_=x_passes[c])
+            raw[c] = raw_c
+
+        def features_to_partitions(slabs, grouped, first_col, tag):
+            bank = psum.tile([P, PAIR, 2 * P], F32, tag=tag, name="bank_" + tag)
+            for s, slab in enumerate(slabs):
+                for u in range(PAIR):
+                    nc.tensor.transpose(
+                        out=bank[:, u, s * P : (s + 1) * P],
+                        in_=slab[:, u * P : (u + 1) * P],
+                        identity=ident[:],
+                    )
+            nc.scalar.copy(
+                out=grouped[:].bitcast(F32)[:, first_col : first_col + 2 * P, :],
+                in_=bank[:].rearrange("q u r -> q r u"),
+            )
+
+        w_raw = const.tile([P, OUT_HALVES, N_IN], BF16)
+        nc.sync.dma_start(out=w_raw[:], in_=weight.rearrange("(h p) i -> p h i", p=P))
+        for c in range(LOADS_AHEAD):
+            load(c)
+        abcd = {}
+        for name, source in (("wa", wa), ("wb", wb), ("wc", wc), ("wd", wd)):
+            abcd[name] = const.tile([P, OUT_HALVES, N_IN], BF16, name=name)
+            nc.sync.dma_start(out=abcd[name][:], in_=source.rearrange("(h p) i -> p h i", p=P))
+
+        ident = const.tile([P, P], F32)
+        make_identity(nc, ident[:])
+        ones_bf16 = const.tile([P, 1], BF16)
+        nc.vector.memset(ones_bf16[:], 1.0)
+        ones_f32 = const.tile([P, 1], F32)
+        nc.vector.memset(ones_f32[:], 1.0)
+
+        w_grouped = const.tile([P, N_OUT, PACK], BF16, align_bytes=64)
+        w_words = w_raw[:].bitcast(F32)
+        features_to_partitions([w_words[:, h, :] for h in range(OUT_HALVES)], w_grouped, 0, "t0")
+        w_codes = const.tile([P, N_OUT], U32, align_bytes=64)
+        w_scales = const.tile([P, N_OUT], U8, align_bytes=64)
+        nc.vector.quantize_mx(
+            out=w_codes[:].bitcast(FP8X4),
+            scales=w_scales[:],
+            in_=w_grouped[:].rearrange("q o t -> q (o t)"),
+        )
+
+        corr = [psum.tile([P, N_IN], F32, name="corr%d" % h) for h in range(OUT_HALVES)]
+        y_sum = psum.tile([P, N_OUT], F32)
+        x_sums = psum.tile([P, IN_CHUNKS, PASSES], F32)
+
+        def transpose_x(c):
+            xa_grouped = two.tile([P, K_PASS, PACK], BF16, align_bytes=64)
+            words = raw[c][:].bitcast(F32)
+            for s in range(PACK // 2):
+                features_to_partitions(
+                    [words[:, 2 * s, :], words[:, 2 * s + 1, :]], xa_grouped, s * 2 * P, "t%d" % s
+                )
+            return xa_grouped
+
+        def regroup_x(c):
+            xb_grouped = two.tile([P, N_IN, PACK], BF16, align_bytes=64)
+            nc.vector.tensor_copy(
+                out=xb_grouped[:].rearrange("p (g i) j -> p g j i", i=4),
+                in_=raw[c][:].rearrange("p j (g i) -> p g j i", i=4),
+            )
+            return xb_grouped
+
+        def quantise_x(c, xa_grouped, xb_grouped):
+            xa_codes[c] = two.tile([P, K_PASS], U32, align_bytes=64, name="xa_codes")
+            xa_scales[c] = two.tile([P, K_PASS], U8, align_bytes=64, name="xa_scales")
+            nc.vector.quantize_mx(
+                out=xa_codes[c][:].bitcast(FP8X4),
+                scales=xa_scales[c][:],
+                in_=xa_grouped[:].rearrange("q b t -> q (b t)"),
+            )
+            xb_codes[c] = three.tile([P, N_IN], U32, align_bytes=64, name="xb_codes")
+            xb_scales[c] = three.tile([P, N_IN], U8, align_bytes=64, name="xb_scales")
+            nc.vector.quantize_mx(
+                out=xb_codes[c][:].bitcast(FP8X4),
+                scales=xb_scales[c][:],
+                in_=xb_grouped[:].rearrange("p i j -> p (i j)"),
+            )
+
+        def first_matmul(c):
+            y_banks = [psum.tile([P, PACK, P], F32, name="y%d" % h) for h in range(OUT_HALVES)]
+            for j in range(PACK):
+                rows = slice(j * P, (j + 1) * P)
+                for h in range(OUT_HALVES):
+                    cols = slice(h * P, (h + 1) * P)
+                    nc.tensor.matmul_mx(
+                        out=y_banks[h][:, j, :],
+                        lhsT=xa_codes[c][:, rows].bitcast(FP8X4),
+                        lhsT_scale=xa_scales[c][:, rows],
+                        rhs=w_codes[:, cols].bitcast(FP8X4),
+                        rhs_scale=w_scales[:, cols],
+                        start=True,
+                        stop=True,
+                    )
+            for j in range(PACK):
+                rows = slice(j * P, (j + 1) * P)
+                nc.tensor.matmul_mx(
+                    out=y_sum[:],
+                    lhsT=xa_codes[c][:, rows].bitcast(FP8X4),
+                    lhsT_scale=xa_scales[c][:, rows],
+                    rhs=w_codes[:].bitcast(FP8X4),
+                    rhs_scale=w_scales[:],
+                    start=(c == 0 and j == 0),
+                    stop=(c == PASSES - 1 and j == PACK - 1),
+                )
+            y_grouped[c] = two.tile([P, N_OUT, PACK], BF16, align_bytes=64, name="y_grouped")
+            for h in range(OUT_HALVES):
+                nc.scalar.copy(
+                    out=y_grouped[c][:, h * P : (h + 1) * P, :],
+                    in_=y_banks[h][:].rearrange("p j o -> p o j"),
+                )
+
+        def quantise_y(c):
+            y_codes[c] = two.tile([P, N_OUT], U32, align_bytes=64, name="y_codes")
+            y_scales[c] = two.tile([P, N_OUT], U8, align_bytes=64, name="y_scales")
+            nc.vector.quantize_mx(
+                out=y_codes[c][:].bitcast(FP8X4),
+                scales=y_scales[c][:],
+                in_=y_grouped[c][:].rearrange("p o j -> p (o j)"),
+            )
+
+        def second_matmul(c):
+            for h in range(OUT_HALVES):
+                cols = slice(h * P, (h + 1) * P)
+                nc.tensor.matmul_mx(
+                    out=corr[h][:],
+                    lhsT=y_codes[c][:, cols].bitcast(FP8X4),
+                    lhsT_scale=y_scales[c][:, cols],
+                    rhs=xb_codes[c][:].bitcast(FP8X4),
+                    rhs_scale=xb_scales[c][:],
+                    start=(c == 0),
+                    stop=(c == PASSES - 1),
+                )
+
+        def sum_x(c):
+            for k in range(IN_CHUNKS):
+                for j in range(PACK):
+                    nc.tensor.matmul(
+                        out=x_sums[:, k, c : c + 1],
+                        lhsT=raw[c][:, j, k * P : (k + 1) * P],
+                        rhs=ones_bf16[:],
+                        start=(j == 0),
+                        stop=(j == PACK - 1),
+                    )
+
+        for r in range(PASSES):
+            if r >= 2:
+                quantise_y(r - 2)
+            if r + LOADS_AHEAD < PASSES:
+                load(r + LOADS_AHEAD)
+            xa_grouped = transpose_x(r)
+            xb_grouped = regroup_x(r)
+            if r >= 1:
+                first_matmul(r - 1)
+            quantise_x(r, xa_grouped, xb_grouped)
+            if r >= 2:
+                second_matmul(r - 2)
+            sum_x(r)
+
+        quantise_y(PASSES - 2)
+        first_matmul(PASSES - 1)
+        second_matmul(PASSES - 2)
+
+        x_mean = const.tile([P, IN_CHUNKS], F32)
+        nc.vector.tensor_reduce(out=x_mean[:], in_=x_sums[:], axis=mybir.AxisListType.X, op=ADD)
+        nc.vector.tensor_scalar_mul(out=x_mean[:], in0=x_mean[:], scalar1=1.0 / BATCH)
+        x_mean_rows = psum.tile([P, N_IN], F32, tag="t0")
+        for k in range(IN_CHUNKS):
+            nc.tensor.matmul(
+                out=x_mean_rows[:, k * P : (k + 1) * P],
+                lhsT=x_mean[:, k : k + 1].to_broadcast([P, P]),
+                rhs=ident[:],
+                start=True,
+                stop=True,
+            )
+
+        y_sum_sb = const.tile([P, N_OUT], F32)
+        nc.vector.tensor_copy(out=y_sum_sb[:], in_=y_sum[:])
+        quantise_y(PASSES - 1)
+        y_total = psum.tile([P, OUT_HALVES], F32, tag="t1")
+        for h in range(OUT_HALVES):
+            nc.tensor.matmul(
+                out=y_total[:, h : h + 1],
+                lhsT=y_sum_sb[:, h * P : (h + 1) * P],
+                rhs=ones_f32[:],
+                start=True,
+                stop=True,
+            )
+        second_matmul(PASSES - 1)
+        y_mean = const.tile([P, OUT_HALVES], F32)
+        nc.vector.tensor_scalar_mul(out=y_mean[:], in0=y_total[:], scalar1=1.0 / BATCH)
+
+        rest = const.tile([P, OUT_HALVES, N_IN], F32)
+        term = const.tile([P, OUT_HALVES, N_IN], F32)
+        for h in range(OUT_HALVES):
+            nc.vector.tensor_tensor(
+                out=term[:, h, :], in0=x_mean_rows[:], in1=abcd["wa"][:, h, :], op=MULT
+            )
+            nc.vector.scalar_tensor_tensor(
+                out=rest[:, h, :],
+                in0=abcd["wb"][:, h, :],
+                scalar=y_mean[:, h : h + 1],
+                in1=abcd["wd"][:, h, :],
+                op0=MULT,
+                op1=ADD,
+            )
+            nc.vector.tensor_tensor(out=rest[:, h, :], in0=rest[:, h, :], in1=term[:, h, :], op=ADD)
+        dw = const.tile([P, OUT_HALVES, N_IN], F32)
+        for h in range(OUT_HALVES):
+            nc.vector.scalar_tensor_tensor(
+                out=dw[:, h, :],
+                in0=corr[h][:],
+                scalar=1.0 / BATCH,
+                in1=abcd["wc"][:, h, :],
+                op0=MULT,
+                op1=MULT,
+            )
+            nc.vector.tensor_tensor(out=dw[:, h, :], in0=dw[:, h, :], in1=rest[:, h, :], op=ADD)
+            nc.sync.dma_start(out=out[h * P : (h + 1) * P, :], in_=dw[:, h, :])

@@ -180,8 +180,8 @@ def tile_hebbianlinear_pa_k_kernel(tc, x, wa, wb, wc, wd, weight, out):
                     stop=(c == PASSES - 1),
                 )
 
-        def sum_x(c):
-            for k in range(IN_CHUNKS):
+        def sum_x(c, chunks):
+            for k in chunks:
                 for j in range(PACK):
                     nc.tensor.matmul(
                         out=x_sums[:, k, c : c + 1],
@@ -196,14 +196,15 @@ def tile_hebbianlinear_pa_k_kernel(tc, x, wa, wb, wc, wd, weight, out):
                 quantise_y(r - 2)
             if r + LOADS_AHEAD < PASSES:
                 load(r + LOADS_AHEAD)
+            sum_x(r, range(0, IN_CHUNKS // 2))
             xa_grouped = transpose_x(r)
+            sum_x(r, range(IN_CHUNKS // 2, IN_CHUNKS))
             xb_grouped = regroup_x(r)
             if r >= 1:
                 first_matmul(r - 1)
             quantise_x(r, xa_grouped, xb_grouped)
             if r >= 2:
                 second_matmul(r - 2)
-            sum_x(r)
 
         quantise_y(PASSES - 2)
         first_matmul(PASSES - 1)

@@ -20,6 +20,8 @@ OUT_HALVES = N_OUT // P
 IN_CHUNKS = N_IN // P
 PAIR = 2
 LOADS_AHEAD = 4
+SUMS_AHEAD = 1
+CORR_LAG = 4
 
 FLOPS = 2 * 2 * BATCH * N_IN * N_OUT
 
@@ -32,7 +34,7 @@ def tile_hebbianlinear_pa_k_kernel(tc, x, wa, wb, wc, wd, weight, out):
         const = ctx.enter_context(tc.tile_pool(name="const", bufs=1))
         raw_pool = ctx.enter_context(tc.tile_pool(name="raw", bufs=LOADS_AHEAD + 2))
         two = ctx.enter_context(tc.tile_pool(name="two", bufs=2))
-        three = ctx.enter_context(tc.tile_pool(name="three", bufs=3))
+        late = ctx.enter_context(tc.tile_pool(name="late", bufs=CORR_LAG + 1))
         psum = ctx.enter_context(tc.psum_pool(name="psum", bufs=1))
         ctx.enter_context(tc.manual_schedule())
 
@@ -79,7 +81,7 @@ def tile_hebbianlinear_pa_k_kernel(tc, x, wa, wb, wc, wd, weight, out):
 
         w_grouped = const.tile([P, N_OUT, PACK], BF16, align_bytes=64)
         w_words = w_raw[:].bitcast(F32)
-        features_to_partitions([w_words[:, h, :] for h in range(OUT_HALVES)], w_grouped, 0, "t0")
+        features_to_partitions([w_words[:, h, :] for h in range(OUT_HALVES)], w_grouped, 0, "y0")
         w_codes = const.tile([P, N_OUT], U32, align_bytes=64)
         w_scales = const.tile([P, N_OUT], U8, align_bytes=64)
         nc.vector.quantize_mx(
@@ -117,8 +119,8 @@ def tile_hebbianlinear_pa_k_kernel(tc, x, wa, wb, wc, wd, weight, out):
                 scales=xa_scales[c][:],
                 in_=xa_grouped[:].rearrange("q b t -> q (b t)"),
             )
-            xb_codes[c] = three.tile([P, N_IN], U32, align_bytes=64, name="xb_codes")
-            xb_scales[c] = three.tile([P, N_IN], U8, align_bytes=64, name="xb_scales")
+            xb_codes[c] = late.tile([P, N_IN], U32, align_bytes=64, name="xb_codes")
+            xb_scales[c] = late.tile([P, N_IN], U8, align_bytes=64, name="xb_scales")
             nc.vector.quantize_mx(
                 out=xb_codes[c][:].bitcast(FP8X4),
                 scales=xb_scales[c][:],
@@ -159,8 +161,8 @@ def tile_hebbianlinear_pa_k_kernel(tc, x, wa, wb, wc, wd, weight, out):
                 )
 
         def quantise_y(c):
-            y_codes[c] = two.tile([P, N_OUT], U32, align_bytes=64, name="y_codes")
-            y_scales[c] = two.tile([P, N_OUT], U8, align_bytes=64, name="y_scales")
+            y_codes[c] = late.tile([P, N_OUT], U32, align_bytes=64, name="y_codes")
+            y_scales[c] = late.tile([P, N_OUT], U8, align_bytes=64, name="y_scales")
             nc.vector.quantize_mx(
                 out=y_codes[c][:].bitcast(FP8X4),
                 scales=y_scales[c][:],
@@ -180,8 +182,8 @@ def tile_hebbianlinear_pa_k_kernel(tc, x, wa, wb, wc, wd, weight, out):
                     stop=(c == PASSES - 1),
                 )
 
-        def sum_x(c, chunks):
-            for k in chunks:
+        def sum_x(c):
+            for k in range(IN_CHUNKS):
                 for j in range(PACK):
                     nc.tensor.matmul(
                         out=x_sums[:, k, c : c + 1],
@@ -191,29 +193,30 @@ def tile_hebbianlinear_pa_k_kernel(tc, x, wa, wb, wc, wd, weight, out):
                         stop=(j == PACK - 1),
                     )
 
+        x_mean = const.tile([P, IN_CHUNKS], F32)
+        summed = 0
         for r in range(PASSES):
+            if r == PASSES - SUMS_AHEAD:
+                nc.vector.tensor_reduce(
+                    out=x_mean[:], in_=x_sums[:], axis=mybir.AxisListType.X, op=ADD
+                )
+                nc.vector.tensor_scalar_mul(out=x_mean[:], in0=x_mean[:], scalar1=1.0 / BATCH)
             if r >= 2:
                 quantise_y(r - 2)
             if r + LOADS_AHEAD < PASSES:
                 load(r + LOADS_AHEAD)
-            sum_x(r, range(0, IN_CHUNKS // 2))
             xa_grouped = transpose_x(r)
-            sum_x(r, range(IN_CHUNKS // 2, IN_CHUNKS))
+            while summed < min(r + 1 + SUMS_AHEAD, PASSES):
+                sum_x(summed)
+                summed += 1
             xb_grouped = regroup_x(r)
             if r >= 1:
                 first_matmul(r - 1)
             quantise_x(r, xa_grouped, xb_grouped)
-            if r >= 2:
-                second_matmul(r - 2)
+            if r >= CORR_LAG:
+                second_matmul(r - CORR_LAG)
 
-        quantise_y(PASSES - 2)
-        first_matmul(PASSES - 1)
-        second_matmul(PASSES - 2)
-
-        x_mean = const.tile([P, IN_CHUNKS], F32)
-        nc.vector.tensor_reduce(out=x_mean[:], in_=x_sums[:], axis=mybir.AxisListType.X, op=ADD)
-        nc.vector.tensor_scalar_mul(out=x_mean[:], in0=x_mean[:], scalar1=1.0 / BATCH)
-        x_mean_rows = psum.tile([P, N_IN], F32, tag="t0")
+        x_mean_rows = psum.tile([P, N_IN], F32, tag="x_sums")
         for k in range(IN_CHUNKS):
             nc.tensor.matmul(
                 out=x_mean_rows[:, k * P : (k + 1) * P],
@@ -222,10 +225,24 @@ def tile_hebbianlinear_pa_k_kernel(tc, x, wa, wb, wc, wd, weight, out):
                 start=True,
                 stop=True,
             )
+        quantise_y(PASSES - 2)
+        first_matmul(PASSES - 1)
+
+        rest = const.tile([P, OUT_HALVES, N_IN], F32)
+        for h in range(OUT_HALVES):
+            nc.vector.tensor_tensor(
+                out=rest[:, h, :], in0=x_mean_rows[:], in1=abcd["wa"][:, h, :], op=MULT
+            )
+            nc.gpsimd.tensor_tensor(
+                out=rest[:, h, :], in0=rest[:, h, :], in1=abcd["wd"][:, h, :], op=ADD
+            )
 
         y_sum_sb = const.tile([P, N_OUT], F32)
         nc.vector.tensor_copy(out=y_sum_sb[:], in_=y_sum[:])
         quantise_y(PASSES - 1)
+        owed = list(range(PASSES - CORR_LAG, PASSES))
+        for c in owed[: CORR_LAG // 2]:
+            second_matmul(c)
         y_total = psum.tile([P, OUT_HALVES], F32, tag="t1")
         for h in range(OUT_HALVES):
             nc.tensor.matmul(
@@ -235,25 +252,20 @@ def tile_hebbianlinear_pa_k_kernel(tc, x, wa, wb, wc, wd, weight, out):
                 start=True,
                 stop=True,
             )
-        second_matmul(PASSES - 1)
+        for c in owed[CORR_LAG // 2 :]:
+            second_matmul(c)
         y_mean = const.tile([P, OUT_HALVES], F32)
         nc.vector.tensor_scalar_mul(out=y_mean[:], in0=y_total[:], scalar1=1.0 / BATCH)
-
-        rest = const.tile([P, OUT_HALVES, N_IN], F32)
-        term = const.tile([P, OUT_HALVES, N_IN], F32)
         for h in range(OUT_HALVES):
-            nc.vector.tensor_tensor(
-                out=term[:, h, :], in0=x_mean_rows[:], in1=abcd["wa"][:, h, :], op=MULT
-            )
             nc.vector.scalar_tensor_tensor(
                 out=rest[:, h, :],
                 in0=abcd["wb"][:, h, :],
                 scalar=y_mean[:, h : h + 1],
-                in1=abcd["wd"][:, h, :],
+                in1=rest[:, h, :],
                 op0=MULT,
                 op1=ADD,
             )
-            nc.vector.tensor_tensor(out=rest[:, h, :], in0=rest[:, h, :], in1=term[:, h, :], op=ADD)
+
         dw = const.tile([P, OUT_HALVES, N_IN], F32)
         for h in range(OUT_HALVES):
             nc.vector.scalar_tensor_tensor(

@@ -14,14 +14,18 @@ MULT = mybir.AluOpType.mult
 P = 128
 PACK = 4
 K_PASS = P * PACK
+PAIR = 2
 BATCH, N_IN, N_OUT = 16384, 512, 256
 PASSES = BATCH // K_PASS
 OUT_HALVES = N_OUT // P
 IN_CHUNKS = N_IN // P
-PAIR = 2
+
 LOADS_AHEAD = 4
 SUMS_AHEAD = 1
-CORR_LAG = 4
+FIRST_LAG = 2
+Y_LAG = 3
+CORR_LAG = 5
+ROUNDS = PASSES + CORR_LAG
 
 FLOPS = 2 * 2 * BATCH * N_IN * N_OUT
 
@@ -32,9 +36,7 @@ def tile_hebbianlinear_pa_k_kernel(tc, x, wa, wb, wc, wd, weight, out):
 
     with ExitStack() as ctx:
         const = ctx.enter_context(tc.tile_pool(name="const", bufs=1))
-        raw_pool = ctx.enter_context(tc.tile_pool(name="raw", bufs=LOADS_AHEAD + 2))
-        two = ctx.enter_context(tc.tile_pool(name="two", bufs=2))
-        late = ctx.enter_context(tc.tile_pool(name="late", bufs=CORR_LAG + 1))
+        stream = ctx.enter_context(tc.tile_pool(name="stream", bufs=2))
         psum = ctx.enter_context(tc.psum_pool(name="psum", bufs=1))
         ctx.enter_context(tc.manual_schedule())
 
@@ -45,9 +47,8 @@ def tile_hebbianlinear_pa_k_kernel(tc, x, wa, wb, wc, wd, weight, out):
         y_codes, y_scales = {}, {}
 
         def load(c):
-            raw_c = raw_pool.tile([P, PACK, N_IN], BF16)
-            nc.sync.dma_start(out=raw_c[:], in_=x_passes[c])
-            raw[c] = raw_c
+            raw[c] = stream.tile([P, PACK, N_IN], BF16, name="raw", bufs=LOADS_AHEAD + 2)
+            nc.sync.dma_start(out=raw[c][:], in_=x_passes[c])
 
         def features_to_partitions(slabs, grouped, first_col, tag):
             bank = psum.tile([P, PAIR, 2 * P], F32, tag=tag, name="bank_" + tag)
@@ -94,8 +95,19 @@ def tile_hebbianlinear_pa_k_kernel(tc, x, wa, wb, wc, wd, weight, out):
         y_sum = psum.tile([P, N_OUT], F32)
         x_sums = psum.tile([P, IN_CHUNKS, PASSES], F32)
 
+        def sum_x(c):
+            for k in range(IN_CHUNKS):
+                for j in range(PACK):
+                    nc.tensor.matmul(
+                        out=x_sums[:, k, c : c + 1],
+                        lhsT=raw[c][:, j, k * P : (k + 1) * P],
+                        rhs=ones_bf16[:],
+                        start=(j == 0),
+                        stop=(j == PACK - 1),
+                    )
+
         def transpose_x(c):
-            xa_grouped = two.tile([P, K_PASS, PACK], BF16, align_bytes=64)
+            xa_grouped = stream.tile([P, K_PASS, PACK], BF16, align_bytes=64)
             words = raw[c][:].bitcast(F32)
             for s in range(PACK // 2):
                 features_to_partitions(
@@ -104,7 +116,7 @@ def tile_hebbianlinear_pa_k_kernel(tc, x, wa, wb, wc, wd, weight, out):
             return xa_grouped
 
         def regroup_x(c):
-            xb_grouped = two.tile([P, N_IN, PACK], BF16, align_bytes=64)
+            xb_grouped = stream.tile([P, N_IN, PACK], BF16, align_bytes=64)
             nc.vector.tensor_copy(
                 out=xb_grouped[:].rearrange("p (g i) j -> p g j i", i=4),
                 in_=raw[c][:].rearrange("p j (g i) -> p g j i", i=4),
@@ -112,15 +124,23 @@ def tile_hebbianlinear_pa_k_kernel(tc, x, wa, wb, wc, wd, weight, out):
             return xb_grouped
 
         def quantise_x(c, xa_grouped, xb_grouped):
-            xa_codes[c] = two.tile([P, K_PASS], U32, align_bytes=64, name="xa_codes")
-            xa_scales[c] = two.tile([P, K_PASS], U8, align_bytes=64, name="xa_scales")
+            xa_codes[c] = stream.tile(
+                [P, K_PASS], U32, align_bytes=64, name="xa_codes", bufs=FIRST_LAG + 1
+            )
+            xa_scales[c] = stream.tile(
+                [P, K_PASS], U8, align_bytes=64, name="xa_scales", bufs=FIRST_LAG + 1
+            )
             nc.vector.quantize_mx(
                 out=xa_codes[c][:].bitcast(FP8X4),
                 scales=xa_scales[c][:],
                 in_=xa_grouped[:].rearrange("q b t -> q (b t)"),
             )
-            xb_codes[c] = late.tile([P, N_IN], U32, align_bytes=64, name="xb_codes")
-            xb_scales[c] = late.tile([P, N_IN], U8, align_bytes=64, name="xb_scales")
+            xb_codes[c] = stream.tile(
+                [P, N_IN], U32, align_bytes=64, name="xb_codes", bufs=CORR_LAG + 1
+            )
+            xb_scales[c] = stream.tile(
+                [P, N_IN], U8, align_bytes=64, name="xb_scales", bufs=CORR_LAG + 1
+            )
             nc.vector.quantize_mx(
                 out=xb_codes[c][:].bitcast(FP8X4),
                 scales=xb_scales[c][:],
@@ -128,13 +148,14 @@ def tile_hebbianlinear_pa_k_kernel(tc, x, wa, wb, wc, wd, weight, out):
             )
 
         def first_matmul(c):
-            y_banks = [psum.tile([P, PACK, P], F32, name="y%d" % h) for h in range(OUT_HALVES)]
-            for j in range(PACK):
-                rows = slice(j * P, (j + 1) * P)
-                for h in range(OUT_HALVES):
-                    cols = slice(h * P, (h + 1) * P)
+            y_grouped[c] = stream.tile([P, N_OUT, PACK], BF16, align_bytes=64, name="y_grouped")
+            for h in range(OUT_HALVES):
+                cols = slice(h * P, (h + 1) * P)
+                y_bank = psum.tile([P, PACK, P], F32, tag="y%d" % h, name="y_bank")
+                for j in range(PACK):
+                    rows = slice(j * P, (j + 1) * P)
                     nc.tensor.matmul_mx(
-                        out=y_banks[h][:, j, :],
+                        out=y_bank[:, j, :],
                         lhsT=xa_codes[c][:, rows].bitcast(FP8X4),
                         lhsT_scale=xa_scales[c][:, rows],
                         rhs=w_codes[:, cols].bitcast(FP8X4),
@@ -142,6 +163,9 @@ def tile_hebbianlinear_pa_k_kernel(tc, x, wa, wb, wc, wd, weight, out):
                         start=True,
                         stop=True,
                     )
+                nc.scalar.copy(
+                    out=y_grouped[c][:, cols, :], in_=y_bank[:].rearrange("p j o -> p o j")
+                )
             for j in range(PACK):
                 rows = slice(j * P, (j + 1) * P)
                 nc.tensor.matmul_mx(
@@ -153,16 +177,14 @@ def tile_hebbianlinear_pa_k_kernel(tc, x, wa, wb, wc, wd, weight, out):
                     start=(c == 0 and j == 0),
                     stop=(c == PASSES - 1 and j == PACK - 1),
                 )
-            y_grouped[c] = two.tile([P, N_OUT, PACK], BF16, align_bytes=64, name="y_grouped")
-            for h in range(OUT_HALVES):
-                nc.scalar.copy(
-                    out=y_grouped[c][:, h * P : (h + 1) * P, :],
-                    in_=y_banks[h][:].rearrange("p j o -> p o j"),
-                )
 
         def quantise_y(c):
-            y_codes[c] = late.tile([P, N_OUT], U32, align_bytes=64, name="y_codes")
-            y_scales[c] = late.tile([P, N_OUT], U8, align_bytes=64, name="y_scales")
+            y_codes[c] = stream.tile(
+                [P, N_OUT], U32, align_bytes=64, name="y_codes", bufs=CORR_LAG - Y_LAG + 1
+            )
+            y_scales[c] = stream.tile(
+                [P, N_OUT], U8, align_bytes=64, name="y_scales", bufs=CORR_LAG - Y_LAG + 1
+            )
             nc.vector.quantize_mx(
                 out=y_codes[c][:].bitcast(FP8X4),
                 scales=y_scales[c][:],
@@ -182,89 +204,80 @@ def tile_hebbianlinear_pa_k_kernel(tc, x, wa, wb, wc, wd, weight, out):
                     stop=(c == PASSES - 1),
                 )
 
-        def sum_x(c):
-            for k in range(IN_CHUNKS):
-                for j in range(PACK):
-                    nc.tensor.matmul(
-                        out=x_sums[:, k, c : c + 1],
-                        lhsT=raw[c][:, j, k * P : (k + 1) * P],
-                        rhs=ones_bf16[:],
-                        start=(j == 0),
-                        stop=(j == PACK - 1),
-                    )
-
         x_mean = const.tile([P, IN_CHUNKS], F32)
-        summed = 0
-        for r in range(PASSES):
-            if r == PASSES - SUMS_AHEAD:
-                nc.vector.tensor_reduce(
-                    out=x_mean[:], in_=x_sums[:], axis=mybir.AxisListType.X, op=ADD
+        y_sum_sb = const.tile([P, N_OUT], F32)
+        y_mean = const.tile([P, OUT_HALVES], F32)
+        rest = const.tile([P, OUT_HALVES, N_IN], F32)
+
+        def mean_of_x():
+            nc.vector.tensor_reduce(out=x_mean[:], in_=x_sums[:], axis=mybir.AxisListType.X, op=ADD)
+            nc.vector.tensor_scalar_mul(out=x_mean[:], in0=x_mean[:], scalar1=1.0 / BATCH)
+
+        def x_mean_term():
+            x_mean_rows = psum.tile([P, N_IN], F32, tag="x_sums")
+            for k in range(IN_CHUNKS):
+                nc.tensor.matmul(
+                    out=x_mean_rows[:, k * P : (k + 1) * P],
+                    lhsT=x_mean[:, k : k + 1].to_broadcast([P, P]),
+                    rhs=ident[:],
+                    start=True,
+                    stop=True,
                 )
-                nc.vector.tensor_scalar_mul(out=x_mean[:], in0=x_mean[:], scalar1=1.0 / BATCH)
-            if r >= 2:
-                quantise_y(r - 2)
+            for h in range(OUT_HALVES):
+                nc.vector.tensor_tensor(
+                    out=rest[:, h, :], in0=x_mean_rows[:], in1=abcd["wa"][:, h, :], op=MULT
+                )
+                nc.gpsimd.tensor_tensor(
+                    out=rest[:, h, :], in0=rest[:, h, :], in1=abcd["wd"][:, h, :], op=ADD
+                )
+
+        def y_mean_term():
+            y_total = psum.tile([P, OUT_HALVES], F32, tag="t0")
+            for h in range(OUT_HALVES):
+                nc.tensor.matmul(
+                    out=y_total[:, h : h + 1],
+                    lhsT=y_sum_sb[:, h * P : (h + 1) * P],
+                    rhs=ones_f32[:],
+                    start=True,
+                    stop=True,
+                )
+            nc.vector.tensor_scalar_mul(out=y_mean[:], in0=y_total[:], scalar1=1.0 / BATCH)
+            for h in range(OUT_HALVES):
+                nc.vector.scalar_tensor_tensor(
+                    out=rest[:, h, :],
+                    in0=abcd["wb"][:, h, :],
+                    scalar=y_mean[:, h : h + 1],
+                    in1=rest[:, h, :],
+                    op0=MULT,
+                    op1=ADD,
+                )
+
+        summed = 0
+        for r in range(ROUNDS):
+            if r == PASSES - SUMS_AHEAD:
+                mean_of_x()
+            if 0 <= r - Y_LAG < PASSES:
+                quantise_y(r - Y_LAG)
             if r + LOADS_AHEAD < PASSES:
                 load(r + LOADS_AHEAD)
-            xa_grouped = transpose_x(r)
-            while summed < min(r + 1 + SUMS_AHEAD, PASSES):
+            if r < PASSES:
+                xa_grouped = transpose_x(r)
+                xb_grouped = regroup_x(r)
+            while summed < min(r + SUMS_AHEAD + 1, PASSES):
                 sum_x(summed)
                 summed += 1
-            xb_grouped = regroup_x(r)
-            if r >= 1:
-                first_matmul(r - 1)
-            quantise_x(r, xa_grouped, xb_grouped)
-            if r >= CORR_LAG:
+            if r == PASSES:
+                x_mean_term()
+            if 0 <= r - CORR_LAG:
                 second_matmul(r - CORR_LAG)
-
-        x_mean_rows = psum.tile([P, N_IN], F32, tag="x_sums")
-        for k in range(IN_CHUNKS):
-            nc.tensor.matmul(
-                out=x_mean_rows[:, k * P : (k + 1) * P],
-                lhsT=x_mean[:, k : k + 1].to_broadcast([P, P]),
-                rhs=ident[:],
-                start=True,
-                stop=True,
-            )
-        quantise_y(PASSES - 2)
-        first_matmul(PASSES - 1)
-
-        rest = const.tile([P, OUT_HALVES, N_IN], F32)
-        for h in range(OUT_HALVES):
-            nc.vector.tensor_tensor(
-                out=rest[:, h, :], in0=x_mean_rows[:], in1=abcd["wa"][:, h, :], op=MULT
-            )
-            nc.gpsimd.tensor_tensor(
-                out=rest[:, h, :], in0=rest[:, h, :], in1=abcd["wd"][:, h, :], op=ADD
-            )
-
-        y_sum_sb = const.tile([P, N_OUT], F32)
-        nc.vector.tensor_copy(out=y_sum_sb[:], in_=y_sum[:])
-        quantise_y(PASSES - 1)
-        owed = list(range(PASSES - CORR_LAG, PASSES))
-        for c in owed[: CORR_LAG // 2]:
-            second_matmul(c)
-        y_total = psum.tile([P, OUT_HALVES], F32, tag="t1")
-        for h in range(OUT_HALVES):
-            nc.tensor.matmul(
-                out=y_total[:, h : h + 1],
-                lhsT=y_sum_sb[:, h * P : (h + 1) * P],
-                rhs=ones_f32[:],
-                start=True,
-                stop=True,
-            )
-        for c in owed[CORR_LAG // 2 :]:
-            second_matmul(c)
-        y_mean = const.tile([P, OUT_HALVES], F32)
-        nc.vector.tensor_scalar_mul(out=y_mean[:], in0=y_total[:], scalar1=1.0 / BATCH)
-        for h in range(OUT_HALVES):
-            nc.vector.scalar_tensor_tensor(
-                out=rest[:, h, :],
-                in0=abcd["wb"][:, h, :],
-                scalar=y_mean[:, h : h + 1],
-                in1=rest[:, h, :],
-                op0=MULT,
-                op1=ADD,
-            )
+            if r == ROUNDS - 2:
+                y_mean_term()
+            if 0 <= r - FIRST_LAG < PASSES:
+                first_matmul(r - FIRST_LAG)
+            if r - FIRST_LAG == PASSES - 1:
+                nc.vector.tensor_copy(out=y_sum_sb[:], in_=y_sum[:])
+            if r < PASSES:
+                quantise_x(r, xa_grouped, xb_grouped)
 
         dw = const.tile([P, OUT_HALVES, N_IN], F32)
         for h in range(OUT_HALVES):

@@ -22,8 +22,8 @@ IN_CHUNKS = N_IN // P
 
 LOADS_AHEAD = 4
 SUMS_AHEAD = 1
-FIRST_LAG = 2
-Y_LAG = 3
+FIRST_LAG = 1
+Y_LAG = 2
 CORR_LAG = 5
 ROUNDS = PASSES + CORR_LAG
 

@@ -25,6 +25,7 @@ SUMS_AHEAD = 1
 FIRST_LAG = 1
 Y_LAG = 2
 CORR_LAG = 5
+SCALAR_COLS = 64
 ROUNDS = PASSES + CORR_LAG
 
 FLOPS = 2 * 2 * BATCH * N_IN * N_OUT
@@ -117,10 +118,14 @@ def tile_hebbianlinear_pa_k_kernel(tc, x, wa, wb, wc, wd, weight, out):
 
         def regroup_x(c):
             xb_grouped = stream.tile([P, N_IN, PACK], BF16, align_bytes=64)
-            nc.vector.tensor_copy(
-                out=xb_grouped[:].rearrange("p (g i) j -> p g j i", i=4),
-                in_=raw[c][:].rearrange("p j (g i) -> p g j i", i=4),
-            )
+            for copy, cols in (
+                (nc.scalar.copy, slice(0, SCALAR_COLS)),
+                (nc.vector.tensor_copy, slice(SCALAR_COLS, N_IN)),
+            ):
+                copy(
+                    out=xb_grouped[:, cols, :].rearrange("p (g i) j -> p g j i", i=4),
+                    in_=raw[c][:, :, cols].rearrange("p j (g i) -> p g j i", i=4),
+                )
             return xb_grouped
 
         def quantise_x(c, xa_grouped, xb_grouped):
@@ -261,8 +266,8 @@ def tile_hebbianlinear_pa_k_kernel(tc, x, wa, wb, wc, wd, weight, out):
             if r + LOADS_AHEAD < PASSES:
                 load(r + LOADS_AHEAD)
             if r < PASSES:
-                xa_grouped = transpose_x(r)
                 xb_grouped = regroup_x(r)
+                xa_grouped = transpose_x(r)
             while summed < min(r + SUMS_AHEAD + 1, PASSES):
                 sum_x(summed)
                 summed += 1

from contextlib import ExitStack

import concourse.mybir as mybir
from concourse.masks import make_identity

F32 = mybir.dt.float32
BF16 = mybir.dt.bfloat16
U32 = mybir.dt.uint32
U8 = mybir.dt.uint8
FP8X4 = mybir.dt.float8_e4m3fn_x4
ADD = mybir.AluOpType.add
MULT = mybir.AluOpType.mult

P = 128
PACK = 4
K_PASS = P * PACK
PAIR = 2
BATCH, N_IN, N_OUT = 16384, 512, 256
PASSES = BATCH // K_PASS
OUT_HALVES = N_OUT // P
IN_CHUNKS = N_IN // P

LOADS_AHEAD = 4
SUMS_AHEAD = 1
FIRST_LAG = 1
Y_LAG = 2
CORR_LAG = 5
SCALAR_COLS = 64
ROUNDS = PASSES + CORR_LAG

FLOPS = 2 * 2 * BATCH * N_IN * N_OUT


def tile_hebbianlinear_pa_k_kernel(tc, x, wa, wb, wc, wd, weight, out):
    nc = tc.nc
    x_passes = x.rearrange("(c p j) i -> c p j i", p=P, j=PACK)

    with ExitStack() as ctx:
        const = ctx.enter_context(tc.tile_pool(name="const", bufs=1))
        stream = ctx.enter_context(tc.tile_pool(name="stream", bufs=2))
        psum = ctx.enter_context(tc.psum_pool(name="psum", bufs=1))
        ctx.enter_context(tc.manual_schedule())

        raw = {}
        xa_codes, xa_scales = {}, {}
        xb_codes, xb_scales = {}, {}
        y_grouped = {}
        y_codes, y_scales = {}, {}

        def load(c):
            raw[c] = stream.tile([P, PACK, N_IN], BF16, name="raw", bufs=LOADS_AHEAD + 2)
            nc.sync.dma_start(out=raw[c][:], in_=x_passes[c])

        def features_to_partitions(slabs, grouped, first_col, tag):
            bank = psum.tile([P, PAIR, 2 * P], F32, tag=tag, name="bank_" + tag)
            for s, slab in enumerate(slabs):
                for u in range(PAIR):
                    nc.tensor.transpose(
                        out=bank[:, u, s * P : (s + 1) * P],
                        in_=slab[:, u * P : (u + 1) * P],
                        identity=ident[:],
                    )
            nc.scalar.copy(
                out=grouped[:].bitcast(F32)[:, first_col : first_col + 2 * P, :],
                in_=bank[:].rearrange("q u r -> q r u"),
            )

        w_raw = const.tile([P, OUT_HALVES, N_IN], BF16)
        nc.sync.dma_start(out=w_raw[:], in_=weight.rearrange("(h p) i -> p h i", p=P))
        for c in range(LOADS_AHEAD):
            load(c)
        abcd = {}
        for name, source in (("wa", wa), ("wb", wb), ("wc", wc), ("wd", wd)):
            abcd[name] = const.tile([P, OUT_HALVES, N_IN], BF16, name=name)
            nc.sync.dma_start(out=abcd[name][:], in_=source.rearrange("(h p) i -> p h i", p=P))

        ident = const.tile([P, P], F32)
        make_identity(nc, ident[:])
        ones_bf16 = const.tile([P, 1], BF16)
        nc.vector.memset(ones_bf16[:], 1.0)
        ones_f32 = const.tile([P, 1], F32)
        nc.vector.memset(ones_f32[:], 1.0)

        w_grouped = const.tile([P, N_OUT, PACK], BF16, align_bytes=64)
        w_words = w_raw[:].bitcast(F32)
        features_to_partitions([w_words[:, h, :] for h in range(OUT_HALVES)], w_grouped, 0, "y0")
        w_codes = const.tile([P, N_OUT], U32, align_bytes=64)
        w_scales = const.tile([P, N_OUT], U8, align_bytes=64)
        nc.vector.quantize_mx(
            out=w_codes[:].bitcast(FP8X4),
            scales=w_scales[:],
            in_=w_grouped[:].rearrange("q o t -> q (o t)"),
        )

        corr = [psum.tile([P, N_IN], F32, name="corr%d" % h) for h in range(OUT_HALVES)]
        y_sum = psum.tile([P, N_OUT], F32)
        x_sums = psum.tile([P, IN_CHUNKS, PASSES], F32)

        def sum_x(c):
            for k in range(IN_CHUNKS):
                for j in range(PACK):
                    nc.tensor.matmul(
                        out=x_sums[:, k, c : c + 1],
                        lhsT=raw[c][:, j, k * P : (k + 1) * P],
                        rhs=ones_bf16[:],
                        start=(j == 0),
                        stop=(j == PACK - 1),
                    )

        def transpose_x(c):
            xa_grouped = stream.tile([P, K_PASS, PACK], BF16, align_bytes=64)
            words = raw[c][:].bitcast(F32)
            for s in range(PACK // 2):
                features_to_partitions(
                    [words[:, 2 * s, :], words[:, 2 * s + 1, :]], xa_grouped, s * 2 * P, "t%d" % s
                )
            return xa_grouped

        def regroup_x(c):
            xb_grouped = stream.tile([P, N_IN, PACK], BF16, align_bytes=64)
            for copy, cols in (
                (nc.scalar.copy, slice(0, SCALAR_COLS)),
                (nc.vector.tensor_copy, slice(SCALAR_COLS, N_IN)),
            ):
                copy(
                    out=xb_grouped[:, cols, :].rearrange("p (g i) j -> p g j i", i=4),
                    in_=raw[c][:, :, cols].rearrange("p j (g i) -> p g j i", i=4),
                )
            return xb_grouped

        def quantise_x(c, xa_grouped, xb_grouped):
            xa_codes[c] = stream.tile(
                [P, K_PASS], U32, align_bytes=64, name="xa_codes", bufs=FIRST_LAG + 1
            )
            xa_scales[c] = stream.tile(
                [P, K_PASS], U8, align_bytes=64, name="xa_scales", bufs=FIRST_LAG + 1
            )
            nc.vector.quantize_mx(
                out=xa_codes[c][:].bitcast(FP8X4),
                scales=xa_scales[c][:],
                in_=xa_grouped[:].rearrange("q b t -> q (b t)"),
            )
            xb_codes[c] = stream.tile(
                [P, N_IN], U32, align_bytes=64, name="xb_codes", bufs=CORR_LAG + 1
            )
            xb_scales[c] = stream.tile(
                [P, N_IN], U8, align_bytes=64, name="xb_scales", bufs=CORR_LAG + 1
            )
            nc.vector.quantize_mx(
                out=xb_codes[c][:].bitcast(FP8X4),
                scales=xb_scales[c][:],
                in_=xb_grouped[:].rearrange("p i j -> p (i j)"),
            )

        def first_matmul(c):
            y_grouped[c] = stream.tile([P, N_OUT, PACK], BF16, align_bytes=64, name="y_grouped")
            for h in range(OUT_HALVES):
                cols = slice(h * P, (h + 1) * P)
                y_bank = psum.tile([P, PACK, P], F32, tag="y%d" % h, name="y_bank")
                for j in range(PACK):
                    rows = slice(j * P, (j + 1) * P)
                    nc.tensor.matmul_mx(
                        out=y_bank[:, j, :],
                        lhsT=xa_codes[c][:, rows].bitcast(FP8X4),
                        lhsT_scale=xa_scales[c][:, rows],
                        rhs=w_codes[:, cols].bitcast(FP8X4),
                        rhs_scale=w_scales[:, cols],
                        start=True,
                        stop=True,
                    )
                nc.scalar.copy(
                    out=y_grouped[c][:, cols, :], in_=y_bank[:].rearrange("p j o -> p o j")
                )
            for j in range(PACK):
                rows = slice(j * P, (j + 1) * P)
                nc.tensor.matmul_mx(
                    out=y_sum[:],
                    lhsT=xa_codes[c][:, rows].bitcast(FP8X4),
                    lhsT_scale=xa_scales[c][:, rows],
                    rhs=w_codes[:].bitcast(FP8X4),
                    rhs_scale=w_scales[:],
                    start=(c == 0 and j == 0),
                    stop=(c == PASSES - 1 and j == PACK - 1),
                )

        def quantise_y(c):
            y_codes[c] = stream.tile(
                [P, N_OUT], U32, align_bytes=64, name="y_codes", bufs=CORR_LAG - Y_LAG + 1
            )
            y_scales[c] = stream.tile(
                [P, N_OUT], U8, align_bytes=64, name="y_scales", bufs=CORR_LAG - Y_LAG + 1
            )
            nc.vector.quantize_mx(
                out=y_codes[c][:].bitcast(FP8X4),
                scales=y_scales[c][:],
                in_=y_grouped[c][:].rearrange("p o j -> p (o j)"),
            )

        def second_matmul(c):
            for h in range(OUT_HALVES):
                cols = slice(h * P, (h + 1) * P)
                nc.tensor.matmul_mx(
                    out=corr[h][:],
                    lhsT=y_codes[c][:, cols].bitcast(FP8X4),
                    lhsT_scale=y_scales[c][:, cols],
                    rhs=xb_codes[c][:].bitcast(FP8X4),
                    rhs_scale=xb_scales[c][:],
                    start=(c == 0),
                    stop=(c == PASSES - 1),
                )

        x_mean = const.tile([P, IN_CHUNKS], F32)
        y_sum_sb = const.tile([P, N_OUT], F32)
        y_mean = const.tile([P, OUT_HALVES], F32)
        rest = const.tile([P, OUT_HALVES, N_IN], F32)

        def mean_of_x():
            nc.vector.tensor_reduce(out=x_mean[:], in_=x_sums[:], axis=mybir.AxisListType.X, op=ADD)
            nc.vector.tensor_scalar_mul(out=x_mean[:], in0=x_mean[:], scalar1=1.0 / BATCH)

        def x_mean_term():
            x_mean_rows = psum.tile([P, N_IN], F32, tag="x_sums")
            for k in range(IN_CHUNKS):
                nc.tensor.matmul(
                    out=x_mean_rows[:, k * P : (k + 1) * P],
                    lhsT=x_mean[:, k : k + 1].to_broadcast([P, P]),
                    rhs=ident[:],
                    start=True,
                    stop=True,
                )
            for h in range(OUT_HALVES):
                nc.vector.tensor_tensor(
                    out=rest[:, h, :], in0=x_mean_rows[:], in1=abcd["wa"][:, h, :], op=MULT
                )
                nc.gpsimd.tensor_tensor(
                    out=rest[:, h, :], in0=rest[:, h, :], in1=abcd["wd"][:, h, :], op=ADD
                )

        def y_mean_term():
            y_total = psum.tile([P, OUT_HALVES], F32, tag="t0")
            for h in range(OUT_HALVES):
                nc.tensor.matmul(
                    out=y_total[:, h : h + 1],
                    lhsT=y_sum_sb[:, h * P : (h + 1) * P],
                    rhs=ones_f32[:],
                    start=True,
                    stop=True,
                )
            nc.vector.tensor_scalar_mul(out=y_mean[:], in0=y_total[:], scalar1=1.0 / BATCH)
            for h in range(OUT_HALVES):
                nc.vector.scalar_tensor_tensor(
                    out=rest[:, h, :],
                    in0=abcd["wb"][:, h, :],
                    scalar=y_mean[:, h : h + 1],
                    in1=rest[:, h, :],
                    op0=MULT,
                    op1=ADD,
                )

        summed = 0
        for r in range(ROUNDS):
            if r == PASSES - SUMS_AHEAD:
                mean_of_x()
            if 0 <= r - Y_LAG < PASSES:
                quantise_y(r - Y_LAG)
            if r + LOADS_AHEAD < PASSES:
                load(r + LOADS_AHEAD)
            if r < PASSES:
                xb_grouped = regroup_x(r)
                xa_grouped = transpose_x(r)
            while summed < min(r + SUMS_AHEAD + 1, PASSES):
                sum_x(summed)
                summed += 1
            if r == PASSES:
                x_mean_term()
            if 0 <= r - CORR_LAG:
                second_matmul(r - CORR_LAG)
            if r == ROUNDS - 2:
                y_mean_term()
            if 0 <= r - FIRST_LAG < PASSES:
                first_matmul(r - FIRST_LAG)
            if r - FIRST_LAG == PASSES - 1:
                nc.vector.tensor_copy(out=y_sum_sb[:], in_=y_sum[:])
            if r < PASSES:
                quantise_x(r, xa_grouped, xb_grouped)

        dw = const.tile([P, OUT_HALVES, N_IN], F32)
        for h in range(OUT_HALVES):
            nc.vector.scalar_tensor_tensor(
                out=dw[:, h, :],
                in0=corr[h][:],
                scalar=1.0 / BATCH,
                in1=abcd["wc"][:, h, :],
                op0=MULT,
                op1=MULT,
            )
            nc.vector.tensor_tensor(out=dw[:, h, :], in0=dw[:, h, :], in1=rest[:, h, :], op=ADD)
            nc.sync.dma_start(out=out[h * P : (h + 1) * P, :], in_=dw[:, h, :])
